import numpy as np
import ml_dtypes


def mxq(x, axis, fmt="e4m3"):
    dtype, down = {"e4m3": (ml_dtypes.float8_e4m3fn, 7), "e5m2": (ml_dtypes.float8_e5m2, 14)}[fmt]
    v = np.moveaxis(np.asarray(x, np.float32).astype(ml_dtypes.bfloat16).astype(np.float64), axis, -1)
    blocks = v.reshape(v.shape[:-1] + (-1, 32))
    amax = np.abs(blocks).max(-1, keepdims=True)
    byte = np.maximum(np.where(amax > 0, np.frexp(amax)[1] - 1 + 127, 0) - down, 1)
    scale = np.exp2(byte - 127.0)
    codes = (blocks / scale).astype(np.float32).astype(dtype).astype(np.float64)
    return np.moveaxis((codes * scale).reshape(v.shape), -1, axis)


WIDE = False


def mx_kscale(k):
    if not WIDE:
        return np.ones(k)
    levels = np.array([10, -10, 5, -5, 0])
    if k % 512:
        return np.exp2(np.random.permutation(np.resize(levels, k // 32))).repeat(32)
    a = np.empty((k // 512, 16))
    for p in range(k // 512):
        a[p, :8] = np.random.permutation(np.resize(levels, 8))
        for g in range(8):
            far = levels[np.abs(levels - a[p, g]) >= 10]
            a[p, g + 8] = far[np.random.randint(len(far))]
    return np.exp2(a.ravel()).repeat(32)


BF16 = ml_dtypes.bfloat16


def bf(x):
    return np.asarray(x, np.float32).astype(BF16)


def f64(x):
    return np.asarray(x).astype(np.float64)


B, F, D, L1, L2, L3 = 16, 64, 32, 256, 256, 512
H2 = L2 // 2
K3 = H2 * F
T = B * D


def interact(h, x0):
    z = h.transpose(0, 2, 1)[:, :, :, None] * x0.transpose(0, 2, 1)[:, :, None, :]
    return z.reshape(z.shape[0], z.shape[1], -1)


def setup_inputs():
    a = mx_kscale(T).reshape(B, D)[:, 0]
    u = mx_kscale(L3)
    h0 = bf(np.maximum(np.random.standard_normal((B, H2, D)) * 0.75, 0.0))
    x0 = bf(np.random.standard_normal((B, F, D)))
    W0 = bf(np.random.standard_normal((K3, L3)) / np.sqrt(K3))
    b3 = bf(np.random.standard_normal(L3) * 0.2)
    g = bf(np.random.standard_normal((B, L3)) * np.exp2(np.random.randint(-6, 1, (B, 1))) * 4.0 / a[:, None] * u[None, :])
    pre = interact(f64(h0), f64(x0)) @ f64(W0) + f64(b3)
    return {"h2": bf(f64(h0) * a[:, None, None]), "x0": x0, "W3": bf(f64(W0) / u[None, :]), "b3": b3,
            "pre": np.asarray(pre, np.float32), "grad_out": g}


def reference(h2, x0, W3, b3, pre, grad_out):
    xf = f64(x0)
    z = interact(f64(h2), xf).reshape(T, K3)
    dp = (f64(grad_out)[:, None, :] * (f64(pre) > 0.0)).reshape(T, L3)
    dz = mxq(dp, 1, "e5m2") @ mxq(f64(W3), 1, "e4m3").T
    dh = (dz.reshape(B, D, H2, F) * xf.transpose(0, 2, 1)[:, :, None, :]).sum(axis=3).transpose(0, 2, 1)
    dw = mxq(z, 0, "e4m3").T @ mxq(dp, 0, "e5m2")
    return dh, dw

@@ -1,0 +1,260 @@
+from contextlib import ExitStack
+
+import concourse.mybir as mybir
+from concourse.masks import make_identity
+
+NB, NF, NG, ND, NC = 16, 128, 64, 32, 512
+NT = NB * ND
+NK = NF * NG
+FLOPS = 2 * 2 * NT * NC * NK
+BYTES = 2 * (NB * NF * ND + NB * NG * ND + NK * NC + NB * NC) + 4 * (NT * NC + NB * NF * ND + NK * NC)
+
+F32 = mybir.dt.float32
+BF16 = mybir.dt.bfloat16
+U32 = mybir.dt.uint32
+U8 = mybir.dt.uint8
+E4X4 = mybir.dt.float8_e4m3fn_x4
+E5X4 = mybir.dt.float8_e5m2_x4
+MULT = mybir.AluOpType.mult
+ADD = mybir.AluOpType.add
+IS_GT = mybir.AluOpType.is_gt
+
+P = 128
+GG = 4
+NGRP = NG // GG
+WIDE = GG * P * 4
+LOADS_AHEAD = 8
+TURNS_AHEAD = 2
+
+
+def tile_cin_pb_v_kernel(tc, h2, x0, W3, b3, pre, grad_out, out_0, out_1):
+    nc = tc.nc
+    w3_v = W3.rearrange("(f g) c -> f g c", g=NG)
+    out1_v = out_1.rearrange("(f g) c -> f g c", g=NG)
+    pre_v = pre.rearrange("b (q j) c -> (b q) j c", j=4)
+
+    with ExitStack() as ctx:
+        const = ctx.enter_context(tc.tile_pool(name="const", bufs=1))
+        st3 = ctx.enter_context(tc.tile_pool(name="st3", bufs=3))
+        st2 = ctx.enter_context(tc.tile_pool(name="st2", bufs=2))
+        ps_tr = ctx.enter_context(tc.psum_pool(name="ps_tr", bufs=2))
+        ps_az = ctx.enter_context(tc.psum_pool(name="ps_az", bufs=4))
+        ps_bw = ctx.enter_context(tc.psum_pool(name="ps_bw", bufs=2))
+        ctx.enter_context(tc.manual_schedule())
+
+        ident = const.tile([P, P], F32, name="ident")
+        spread = const.tile([P, P], BF16, name="spread")
+        gr = const.tile([P, NC], BF16, name="gr")
+        h2f = const.tile([P, NT], BF16, name="h2f")
+        x0f = const.tile([P, NT], BF16, name="x0f")
+        h2t = const.tile([P, NF * 4], BF16, name="h2t")
+        x0t = const.tile([P, NG * 4], BF16, name="x0t")
+        pre_sb = const.tile([P, 4, NC], F32, name="pre_sb")
+        dp_nat = const.tile([P, 4, NC], BF16, name="dp_nat")
+        dp_tok = const.tile([P, WIDE], BF16, name="dp_tok", align_bytes=64)
+        dp_ftr = const.tile([P, WIDE], BF16, name="dp_ftr", align_bytes=64)
+        dpk_c = const.tile([P, NC], U32, name="dpk_c", align_bytes=64)
+        dpk_s = const.tile([P, NC], U8, name="dpk_s", align_bytes=64)
+        dpf_c = const.tile([P, NT], U32, name="dpf_c", align_bytes=64)
+        dpf_s = const.tile([P, NT], U8, name="dpf_s", align_bytes=64)
+        o0 = const.tile([P, NT], F32, name="o0")
+        acc = []
+        for j in range(4):
+            acc_j = const.tile([P, NF], F32, name="acc%d" % j)
+            acc.append(acc_j)
+        w_raw = []
+        for i in range(NGRP):
+            w_i = const.tile([P, GG, NC], BF16, name="w_raw%d" % i)
+            w_raw.append(w_i)
+
+        x0t_v = x0t[:].rearrange("p (g j) -> p g j", j=4)
+        h2t_v = h2t[:].rearrange("p (f j) -> p f j", j=4)
+
+        def load_w(i):
+            nc.sync.dma_start(out=w_raw[i][:], in_=w3_v[:, GG * i : GG * (i + 1), :])
+
+        def turn(src, dst, pool, tag):
+            words = src.rearrange("p g c -> p (g c)").bitcast(F32)
+            dwords = dst.bitcast(F32)
+            for h in range(2):
+                bank = pool.tile([P, 512], F32, name=tag, tag=tag)
+                for k in range(4):
+                    g = 2 * h + k // 2
+                    u = k % 2
+                    nc.tensor.transpose(
+                        out=bank[:, P * k : P * (k + 1)],
+                        in_=words[:, 256 * g + u : 256 * (g + 1) : 2],
+                        identity=ident[:],
+                    )
+                nc.scalar.copy(
+                    out=dwords[:, 512 * h : 512 * (h + 1)].rearrange("q (g f u) -> q g f u", g=2, u=2),
+                    in_=bank[:].rearrange("q (g u f) -> q g f u", g=2, u=2),
+                )
+
+        gw = {}
+        wc = {}
+        zs = {}
+        zc = {}
+        az = {}
+
+        def turn_w(i):
+            gw_t = st3.tile([P, WIDE], BF16, name="gw", tag="gw", align_bytes=64)
+            gw[i] = gw_t
+            turn(w_raw[i][:], gw_t[:], ps_tr, "tr")
+
+        def quant_w(i):
+            wc_t = st2.tile([P, 512], U32, name="wc", tag="wc", align_bytes=64)
+            ws_t = st2.tile([P, 512], U8, name="ws", tag="ws", align_bytes=64)
+            wc[i] = (wc_t, ws_t)
+            nc.vector.quantize_mx(out=wc_t[:].bitcast(E4X4), scales=ws_t[:], in_=gw.pop(i)[:])
+
+        def mm_a(i):
+            wc_t, ws_t = wc.pop(i)
+            banks = []
+            for j in range(4):
+                az_t = ps_az.tile([P, 512], F32, name="az", tag="az")
+                banks.append(az_t)
+                nc.tensor.matmul_mx(
+                    out=az_t[:],
+                    lhsT=dpf_c[:, P * j : P * (j + 1)].bitcast(E5X4),
+                    lhsT_scale=dpf_s[:, P * j : P * (j + 1)],
+                    rhs=wc_t[:].bitcast(E4X4),
+                    rhs_scale=ws_t[:],
+                    start=True,
+                    stop=True,
+                )
+            az[i] = banks
+
+        def fold(i):
+            banks = az.pop(i)
+            for s in range(GG):
+                g = GG * i + s
+                for j in range(4):
+                    if g == 0:
+                        nc.vector.tensor_scalar(
+                            out=acc[j][:],
+                            in0=banks[j][:, 0:P],
+                            scalar1=x0t_v[:, 0, j : j + 1],
+                            scalar2=None,
+                            op0=MULT,
+                        )
+                    else:
+                        nc.vector.scalar_tensor_tensor(
+                            out=acc[j][:],
+                            in0=banks[j][:, P * s : P * (s + 1)],
+                            scalar=x0t_v[:, g, j : j + 1],
+                            in1=acc[j][:],
+                            op0=MULT,
+                            op1=ADD,
+                        )
+
+        def make_z(i):
+            zs_t = st2.tile([P, WIDE], BF16, name="zs", tag="zs", align_bytes=64)
+            zs[i] = zs_t
+            nc.vector.tensor_tensor(
+                out=zs_t[:].rearrange("p (g f j) -> p g f j", g=GG, j=4),
+                in0=x0t_v[:, GG * i : GG * (i + 1), :].unsqueeze(2).to_broadcast([P, GG, NF, 4]),
+                in1=h2t_v.unsqueeze(1).to_broadcast([P, GG, NF, 4]),
+                op=MULT,
+            )
+
+        def quant_z(i):
+            zc_t = st3.tile([P, 512], U32, name="zc", tag="zc", align_bytes=64)
+            zq_t = st3.tile([P, 512], U8, name="zq", tag="zq", align_bytes=64)
+            zc[i] = (zc_t, zq_t)
+            nc.vector.quantize_mx(out=zc_t[:].bitcast(E4X4), scales=zq_t[:], in_=zs.pop(i)[:])
+
+        def mm_b(i):
+            zc_t, zq_t = zc.pop(i)
+            ot = st3.tile([P, GG, NC], F32, name="ot", tag="ot")
+            for s in range(GG):
+                bw = ps_bw.tile([P, 512], F32, name="bw", tag="bw")
+                nc.tensor.matmul_mx(
+                    out=bw[:],
+                    lhsT=zc_t[:, P * s : P * (s + 1)].bitcast(E4X4),
+                    lhsT_scale=zq_t[:, P * s : P * (s + 1)],
+                    rhs=dpk_c[:].bitcast(E5X4),
+                    rhs_scale=dpk_s[:],
+                    start=True,
+                    stop=True,
+                )
+                nc.scalar.copy(out=ot[:, s, :], in_=bw[:])
+            nc.sync.dma_start(out=out1_v[:, GG * i : GG * (i + 1), :], in_=ot[:])
+
+        make_identity(nc, ident[:])
+        nc.vector.memset(gr[:], 0.0)
+        x0_v = x0.rearrange("b g d -> g b d")
+        nc.sync.dma_start(out=x0f[0:NG, :].rearrange("g (b d) -> g b d", d=ND), in_=x0_v)
+        nc.sync.dma_start(out=x0f[NG:P, :].rearrange("g (b d) -> g b d", d=ND), in_=x0_v)
+        nc.sync.dma_start(out=h2f[:].rearrange("f (b d) -> f b d", d=ND), in_=h2.rearrange("b f d -> f b d"))
+        nc.sync.dma_start(out=gr[0:NB, :], in_=grad_out)
+        for j in range(4):
+            nc.sync.dma_start(out=pre_sb[:, j, :], in_=pre_v[:, j, :])
+        for i in range(LOADS_AHEAD):
+            load_w(i)
+
+        nc.vector.tensor_copy(
+            out=spread[:].rearrange("k (b r) -> k b r", r=8),
+            in_=ident[:, 0:NB].unsqueeze(2).to_broadcast([P, NB, 8]),
+        )
+        hx = ps_bw.tile([P, 512], F32, name="bw", tag="bw")
+        h2w = h2f[:].bitcast(F32)
+        x0w = x0f[:].bitcast(F32)
+        for u in range(2):
+            nc.tensor.transpose(out=hx[:, P * u : P * (u + 1)], in_=h2w[:, u:256:2], identity=ident[:])
+        for u in range(2):
+            nc.tensor.transpose(out=hx[:, P * (2 + u) : P * (3 + u)], in_=x0w[:, u:256:2], identity=ident[:])
+        nc.vector.tensor_copy(
+            out=h2t[:].bitcast(F32).rearrange("p (f u) -> p f u", u=2),
+            in_=hx[:, 0:256].rearrange("p (u f) -> p f u", u=2),
+        )
+        nc.vector.tensor_copy(
+            out=x0t[:].bitcast(F32).rearrange("p (g u) -> p g u", u=2),
+            in_=hx[:, 256:512].rearrange("p (u f) -> p f u", u=2)[:, 0:NG, :],
+        )
+        gps = ps_bw.tile([P, 512], F32, name="bw", tag="bw")
+        nc.tensor.matmul(out=gps[:], lhsT=spread[:], rhs=gr[:], start=True, stop=True)
+        for j in range(4):
+            nc.vector.scalar_tensor_tensor(
+                out=dp_nat[:, j, :],
+                in0=pre_sb[:, j, :],
+                scalar=0.0,
+                in1=gps[:],
+                op0=IS_GT,
+                op1=MULT,
+            )
+        turn(dp_nat[:], dp_ftr[:], ps_az, "az")
+        nc.vector.tensor_copy(
+            out=dp_tok[:].rearrange("p (c j) -> p c j", j=4),
+            in_=dp_nat[:].rearrange("p j c -> p c j"),
+        )
+        make_z(0)
+        turn_w(0)
+        nc.vector.quantize_mx(out=dpf_c[:].bitcast(E5X4), scales=dpf_s[:], in_=dp_ftr[:])
+        nc.vector.quantize_mx(out=dpk_c[:].bitcast(E5X4), scales=dpk_s[:], in_=dp_tok[:])
+        turn_w(1)
+        quant_w(0)
+        mm_a(0)
+
+        for i in range(NGRP):
+            if i + LOADS_AHEAD < NGRP:
+                load_w(i + LOADS_AHEAD)
+            if i + 1 < NGRP:
+                quant_w(i + 1)
+            quant_z(i)
+            if i + TURNS_AHEAD < NGRP:
+                turn_w(i + TURNS_AHEAD)
+            mm_b(i)
+            fold(i)
+            if i + 1 < NGRP:
+                mm_a(i + 1)
+                make_z(i + 1)
+
+        fin = ps_tr.tile([P, 512], F32, name="tr", tag="tr")
+        for j in range(4):
+            nc.tensor.transpose(out=fin[:, P * j : P * (j + 1)], in_=acc[j][:], identity=ident[:])
+        nc.vector.tensor_copy(
+            out=o0[:].rearrange("f (p j) -> f p j", j=4),
+            in_=fin[:].rearrange("f (j p) -> f p j", j=4),
+        )
+        nc.sync.dma_start(out=out_0.rearrange("b f d -> f b d"), in_=o0[:].rearrange("f (b d) -> f b d", d=ND))

@@ -25,6 +25,7 @@ NGRP = NG // GG
 WIDE = GG * P * 4
 LOADS_AHEAD = 8
 TURNS_AHEAD = 2
+GV = 2
 
 
 def tile_cin_pb_v_kernel(tc, h2, x0, W3, b3, pre, grad_out, out_0, out_1):
@@ -59,9 +60,9 @@ def tile_cin_pb_v_kernel(tc, h2, x0, W3, b3, pre, grad_out, out_0, out_1):
         dpf_s = const.tile([P, NT], U8, name="dpf_s", align_bytes=64)
         o0 = const.tile([P, NT], F32, name="o0")
         acc = []
-        for j in range(4):
-            acc_j = const.tile([P, NF], F32, name="acc%d" % j)
-            acc.append(acc_j)
+        for k in range(8):
+            acc_k = const.tile([P, NF], F32, name="acc%d" % k)
+            acc.append(acc_k)
         w_raw = []
         for i in range(NGRP):
             w_i = const.tile([P, GG, NC], BF16, name="w_raw%d" % i)
@@ -108,12 +109,11 @@ def tile_cin_pb_v_kernel(tc, h2, x0, W3, b3, pre, grad_out, out_0, out_1):
             wc[i] = (wc_t, ws_t)
             nc.vector.quantize_mx(out=wc_t[:].bitcast(E4X4), scales=ws_t[:], in_=gw.pop(i)[:])
 
-        def mm_a(i):
-            wc_t, ws_t = wc.pop(i)
-            banks = []
-            for j in range(4):
+        def mm_a(i, js):
+            wc_t, ws_t = wc[i]
+            for j in js:
                 az_t = ps_az.tile([P, 512], F32, name="az", tag="az")
-                banks.append(az_t)
+                az[(i, j)] = az_t
                 nc.tensor.matmul_mx(
                     out=az_t[:],
                     lhsT=dpf_c[:, P * j : P * (j + 1)].bitcast(E5X4),
@@ -123,38 +123,46 @@ def tile_cin_pb_v_kernel(tc, h2, x0, W3, b3, pre, grad_out, out_0, out_1):
                     start=True,
                     stop=True,
                 )
-            az[i] = banks
 
-        def fold(i):
-            banks = az.pop(i)
+        def fold(i, js):
             for s in range(GG):
                 g = GG * i + s
-                for j in range(4):
-                    if g == 0:
+                for j in js:
+                    a_t = acc[4 * (s % 2) + j]
+                    if g < 2:
                         nc.vector.tensor_scalar(
-                            out=acc[j][:],
-                            in0=banks[j][:, 0:P],
-                            scalar1=x0t_v[:, 0, j : j + 1],
+                            out=a_t[:],
+                            in0=az[(i, j)][:, P * s : P * (s + 1)],
+                            scalar1=x0t_v[:, g, j : j + 1],
                             scalar2=None,
                             op0=MULT,
                         )
                     else:
                         nc.vector.scalar_tensor_tensor(
-                            out=acc[j][:],
-                            in0=banks[j][:, P * s : P * (s + 1)],
+                            out=a_t[:],
+                            in0=az[(i, j)][:, P * s : P * (s + 1)],
                             scalar=x0t_v[:, g, j : j + 1],
-                            in1=acc[j][:],
+                            in1=a_t[:],
                             op0=MULT,
                             op1=ADD,
                         )
 
-        def make_z(i):
+        def make_z_pool(i):
             zs_t = st2.tile([P, WIDE], BF16, name="zs", tag="zs", align_bytes=64)
             zs[i] = zs_t
+            for s in range(GV, GG):
+                nc.gpsimd.tensor_tensor(
+                    out=zs_t[:, 4 * P * s : 4 * P * (s + 1)].rearrange("p (f j) -> p f j", j=4),
+                    in0=x0t_v[:, GG * i + s, :].unsqueeze(1).to_broadcast([P, NF, 4]),
+                    in1=h2t_v,
+                    op=MULT,
+                )
+
+        def make_z_vec(i):
             nc.vector.tensor_tensor(
-                out=zs_t[:].rearrange("p (g f j) -> p g f j", g=GG, j=4),
-                in0=x0t_v[:, GG * i : GG * (i + 1), :].unsqueeze(2).to_broadcast([P, GG, NF, 4]),
-                in1=h2t_v.unsqueeze(1).to_broadcast([P, GG, NF, 4]),
+                out=zs[i][:, 0 : 4 * P * GV].rearrange("p (g f j) -> p g f j", g=GV, j=4),
+                in0=x0t_v[:, GG * i : GG * i + GV, :].unsqueeze(2).to_broadcast([P, GV, NF, 4]),
+                in1=h2t_v.unsqueeze(1).to_broadcast([P, GV, NF, 4]),
                 op=MULT,
             )
 
@@ -184,9 +192,9 @@ def tile_cin_pb_v_kernel(tc, h2, x0, W3, b3, pre, grad_out, out_0, out_1):
         make_identity(nc, ident[:])
         nc.vector.memset(gr[:], 0.0)
         x0_v = x0.rearrange("b g d -> g b d")
-        nc.sync.dma_start(out=x0f[0:NG, :].rearrange("g (b d) -> g b d", d=ND), in_=x0_v)
-        nc.sync.dma_start(out=x0f[NG:P, :].rearrange("g (b d) -> g b d", d=ND), in_=x0_v)
-        nc.sync.dma_start(out=h2f[:].rearrange("f (b d) -> f b d", d=ND), in_=h2.rearrange("b f d -> f b d"))
+        nc.scalar.dma_start(out=x0f[0:NG, :].rearrange("g (b d) -> g b d", d=ND), in_=x0_v)
+        nc.scalar.dma_start(out=x0f[NG:P, :].rearrange("g (b d) -> g b d", d=ND), in_=x0_v)
+        nc.scalar.dma_start(out=h2f[:].rearrange("f (b d) -> f b d", d=ND), in_=h2.rearrange("b f d -> f b d"))
         nc.sync.dma_start(out=gr[0:NB, :], in_=grad_out)
         for j in range(4):
             nc.sync.dma_start(out=pre_sb[:, j, :], in_=pre_v[:, j, :])
@@ -196,21 +204,6 @@ def tile_cin_pb_v_kernel(tc, h2, x0, W3, b3, pre, grad_out, out_0, out_1):
         nc.vector.tensor_copy(
             out=spread[:].rearrange("k (b r) -> k b r", r=8),
             in_=ident[:, 0:NB].unsqueeze(2).to_broadcast([P, NB, 8]),
-        )
-        hx = ps_bw.tile([P, 512], F32, name="bw", tag="bw")
-        h2w = h2f[:].bitcast(F32)
-        x0w = x0f[:].bitcast(F32)
-        for u in range(2):
-            nc.tensor.transpose(out=hx[:, P * u : P * (u + 1)], in_=h2w[:, u:256:2], identity=ident[:])
-        for u in range(2):
-            nc.tensor.transpose(out=hx[:, P * (2 + u) : P * (3 + u)], in_=x0w[:, u:256:2], identity=ident[:])
-        nc.vector.tensor_copy(
-            out=h2t[:].bitcast(F32).rearrange("p (f u) -> p f u", u=2),
-            in_=hx[:, 0:256].rearrange("p (u f) -> p f u", u=2),
-        )
-        nc.vector.tensor_copy(
-            out=x0t[:].bitcast(F32).rearrange("p (g u) -> p g u", u=2),
-            in_=hx[:, 256:512].rearrange("p (u f) -> p f u", u=2)[:, 0:NG, :],
         )
         gps = ps_bw.tile([P, 512], F32, name="bw", tag="bw")
         nc.tensor.matmul(out=gps[:], lhsT=spread[:], rhs=gr[:], start=True, stop=True)
@@ -228,30 +221,52 @@ def tile_cin_pb_v_kernel(tc, h2, x0, W3, b3, pre, grad_out, out_0, out_1):
             out=dp_tok[:].rearrange("p (c j) -> p c j", j=4),
             in_=dp_nat[:].rearrange("p j c -> p c j"),
         )
-        make_z(0)
+        hx = ps_bw.tile([P, 512], F32, name="bw", tag="bw")
+        h2w = h2f[:].bitcast(F32)
+        x0w = x0f[:].bitcast(F32)
+        for u in range(2):
+            nc.tensor.transpose(out=hx[:, P * u : P * (u + 1)], in_=h2w[:, u:256:2], identity=ident[:])
+        for u in range(2):
+            nc.tensor.transpose(out=hx[:, P * (2 + u) : P * (3 + u)], in_=x0w[:, u:256:2], identity=ident[:])
         turn_w(0)
         nc.vector.quantize_mx(out=dpf_c[:].bitcast(E5X4), scales=dpf_s[:], in_=dp_ftr[:])
+        nc.vector.tensor_copy(
+            out=h2t[:].bitcast(F32).rearrange("p (f u) -> p f u", u=2),
+            in_=hx[:, 0:256].rearrange("p (u f) -> p f u", u=2),
+        )
+        nc.vector.tensor_copy(
+            out=x0t[:].bitcast(F32).rearrange("p (g u) -> p g u", u=2),
+            in_=hx[:, 256:512].rearrange("p (u f) -> p f u", u=2)[:, 0:NG, :],
+        )
+        make_z_pool(0)
+        make_z_pool(1)
         nc.vector.quantize_mx(out=dpk_c[:].bitcast(E5X4), scales=dpk_s[:], in_=dp_tok[:])
         turn_w(1)
+        make_z_vec(0)
         quant_w(0)
-        mm_a(0)
+        mm_a(0, (0, 1))
 
         for i in range(NGRP):
             if i + LOADS_AHEAD < NGRP:
                 load_w(i + LOADS_AHEAD)
             if i + 1 < NGRP:
+                make_z_vec(i + 1)
                 quant_w(i + 1)
             quant_z(i)
+            if i + 2 < NGRP:
+                make_z_pool(i + 2)
+            mm_a(i, (2, 3))
             if i + TURNS_AHEAD < NGRP:
                 turn_w(i + TURNS_AHEAD)
             mm_b(i)
-            fold(i)
+            fold(i, (0, 1))
             if i + 1 < NGRP:
-                mm_a(i + 1)
-                make_z(i + 1)
+                mm_a(i + 1, (0, 1))
+            fold(i, (2, 3))
 
         fin = ps_tr.tile([P, 512], F32, name="tr", tag="tr")
         for j in range(4):
+            nc.vector.tensor_tensor(out=acc[j][:], in0=acc[j][:], in1=acc[4 + j][:], op=ADD)
             nc.tensor.transpose(out=fin[:, P * j : P * (j + 1)], in_=acc[j][:], identity=ident[:])
         nc.vector.tensor_copy(
             out=o0[:].rearrange("f (p j) -> f p j", j=4),

@@ -38,9 +38,8 @@ def tile_cin_pb_v_kernel(tc, h2, x0, W3, b3, pre, grad_out, out_0, out_1):
         const = ctx.enter_context(tc.tile_pool(name="const", bufs=1))
         st3 = ctx.enter_context(tc.tile_pool(name="st3", bufs=3))
         st2 = ctx.enter_context(tc.tile_pool(name="st2", bufs=2))
-        ps_tr = ctx.enter_context(tc.psum_pool(name="ps_tr", bufs=2))
+        ps_sx = ctx.enter_context(tc.psum_pool(name="ps_sx", bufs=4))
         ps_az = ctx.enter_context(tc.psum_pool(name="ps_az", bufs=4))
-        ps_bw = ctx.enter_context(tc.psum_pool(name="ps_bw", bufs=2))
         ctx.enter_context(tc.manual_schedule())
 
         ident = const.tile([P, P], F32, name="ident")
@@ -101,7 +100,7 @@ def tile_cin_pb_v_kernel(tc, h2, x0, W3, b3, pre, grad_out, out_0, out_1):
         def turn_w(i):
             gw_t = st3.tile([P, WIDE], BF16, name="gw", tag="gw", align_bytes=64)
             gw[i] = gw_t
-            turn(w_raw[i][:], gw_t[:], ps_tr, "tr")
+            turn(w_raw[i][:], gw_t[:], ps_sx, "sx")
 
         def quant_w(i):
             wc_t = st2.tile([P, 512], U32, name="wc", tag="wc", align_bytes=64)
@@ -172,11 +171,16 @@ def tile_cin_pb_v_kernel(tc, h2, x0, W3, b3, pre, grad_out, out_0, out_1):
             zc[i] = (zc_t, zq_t)
             nc.vector.quantize_mx(out=zc_t[:].bitcast(E4X4), scales=zq_t[:], in_=zs.pop(i)[:])
 
-        def mm_b(i):
-            zc_t, zq_t = zc.pop(i)
-            ot = st3.tile([P, GG, NC], F32, name="ot", tag="ot")
-            for s in range(GG):
-                bw = ps_bw.tile([P, 512], F32, name="bw", tag="bw")
+        ots = {}
+
+        def mm_b(i, ss):
+            zc_t, zq_t = zc[i]
+            if 0 in ss:
+                ot_t = st3.tile([P, GG, NC], F32, name="ot", tag="ot")
+                ots[i] = ot_t
+            ot = ots[i]
+            for s in ss:
+                bw = ps_sx.tile([P, 512], F32, name="sx", tag="sx")
                 nc.tensor.matmul_mx(
                     out=bw[:],
                     lhsT=zc_t[:, P * s : P * (s + 1)].bitcast(E4X4),
@@ -187,7 +191,19 @@ def tile_cin_pb_v_kernel(tc, h2, x0, W3, b3, pre, grad_out, out_0, out_1):
                     stop=True,
                 )
                 nc.scalar.copy(out=ot[:, s, :], in_=bw[:])
-            nc.sync.dma_start(out=out1_v[:, GG * i : GG * (i + 1), :], in_=ot[:])
+            if GG - 1 in ss:
+                nc.sync.dma_start(out=out1_v[:, GG * i : GG * (i + 1), :], in_=ot[:])
+
+        fins = []
+
+        def finish(js):
+            if len(fins) == 0:
+                fin_t = ps_az.tile([P, 512], F32, name="az", tag="az")
+                fins.append(fin_t)
+            for j in js:
+                nc.vector.tensor_tensor(out=acc[j][:], in0=acc[j][:], in1=acc[4 + j][:], op=ADD)
+            for j in js:
+                nc.tensor.transpose(out=fins[0][:, P * j : P * (j + 1)], in_=acc[j][:], identity=ident[:])
 
         make_identity(nc, ident[:])
         nc.vector.memset(gr[:], 0.0)
@@ -205,7 +221,7 @@ def tile_cin_pb_v_kernel(tc, h2, x0, W3, b3, pre, grad_out, out_0, out_1):
             out=spread[:].rearrange("k (b r) -> k b r", r=8),
             in_=ident[:, 0:NB].unsqueeze(2).to_broadcast([P, NB, 8]),
         )
-        gps = ps_bw.tile([P, 512], F32, name="bw", tag="bw")
+        gps = ps_sx.tile([P, 512], F32, name="sx", tag="sx")
         nc.tensor.matmul(out=gps[:], lhsT=spread[:], rhs=gr[:], start=True, stop=True)
         for j in range(4):
             nc.vector.scalar_tensor_tensor(
@@ -221,7 +237,7 @@ def tile_cin_pb_v_kernel(tc, h2, x0, W3, b3, pre, grad_out, out_0, out_1):
             out=dp_tok[:].rearrange("p (c j) -> p c j", j=4),
             in_=dp_nat[:].rearrange("p j c -> p c j"),
         )
-        hx = ps_bw.tile([P, 512], F32, name="bw", tag="bw")
+        hx = ps_sx.tile([P, 512], F32, name="sx", tag="sx")
         h2w = h2f[:].bitcast(F32)
         x0w = x0f[:].bitcast(F32)
         for u in range(2):
@@ -244,6 +260,8 @@ def tile_cin_pb_v_kernel(tc, h2, x0, W3, b3, pre, grad_out, out_0, out_1):
         turn_w(1)
         make_z_vec(0)
         quant_w(0)
+        quant_z(0)
+        make_z_pool(2)
         mm_a(0, (0, 1))
 
         for i in range(NGRP):
@@ -252,24 +270,24 @@ def tile_cin_pb_v_kernel(tc, h2, x0, W3, b3, pre, grad_out, out_0, out_1):
             if i + 1 < NGRP:
                 make_z_vec(i + 1)
                 quant_w(i + 1)
-            quant_z(i)
-            if i + 2 < NGRP:
-                make_z_pool(i + 2)
-            mm_a(i, (2, 3))
+                quant_z(i + 1)
+            if i + 3 < NGRP:
+                make_z_pool(i + 3)
             if i + TURNS_AHEAD < NGRP:
                 turn_w(i + TURNS_AHEAD)
-            mm_b(i)
+            mm_b(i, (0, 1))
+            mm_a(i, (2, 3))
+            mm_b(i, (2, 3))
             fold(i, (0, 1))
             if i + 1 < NGRP:
                 mm_a(i + 1, (0, 1))
+            else:
+                finish((0, 1))
             fold(i, (2, 3))
 
-        fin = ps_tr.tile([P, 512], F32, name="tr", tag="tr")
-        for j in range(4):
-            nc.vector.tensor_tensor(out=acc[j][:], in0=acc[j][:], in1=acc[4 + j][:], op=ADD)
-            nc.tensor.transpose(out=fin[:, P * j : P * (j + 1)], in_=acc[j][:], identity=ident[:])
+        finish((2, 3))
         nc.vector.tensor_copy(
             out=o0[:].rearrange("f (p j) -> f p j", j=4),
-            in_=fin[:].rearrange("f (j p) -> f p j", j=4),
+            in_=fins[0][:].rearrange("f (j p) -> f p j", j=4),
         )
         nc.sync.dma_start(out=out_0.rearrange("b f d -> f b d"), in_=o0[:].rearrange("f (b d) -> f b d", d=ND))

@@ -18,6 +18,7 @@ E5X4 = mybir.dt.float8_e5m2_x4
 MULT = mybir.AluOpType.mult
 ADD = mybir.AluOpType.add
 IS_GT = mybir.AluOpType.is_gt
+COPY = mybir.ActivationFunctionType.Copy
 
 P = 128
 GG = 4
@@ -25,7 +26,8 @@ NGRP = NG // GG
 WIDE = GG * P * 4
 LOADS_AHEAD = 8
 TURNS_AHEAD = 2
-GV = 2
+GV = 3
+JS = 3
 
 
 def tile_cin_pb_v_kernel(tc, h2, x0, W3, b3, pre, grad_out, out_0, out_1):
@@ -39,7 +41,8 @@ def tile_cin_pb_v_kernel(tc, h2, x0, W3, b3, pre, grad_out, out_0, out_1):
         st3 = ctx.enter_context(tc.tile_pool(name="st3", bufs=3))
         st2 = ctx.enter_context(tc.tile_pool(name="st2", bufs=2))
         ps_sx = ctx.enter_context(tc.psum_pool(name="ps_sx", bufs=4))
-        ps_az = ctx.enter_context(tc.psum_pool(name="ps_az", bufs=4))
+        ps_az = ctx.enter_context(tc.psum_pool(name="ps_az", bufs=3))
+        ps_ac = ctx.enter_context(tc.psum_pool(name="ps_ac", bufs=1))
         ctx.enter_context(tc.manual_schedule())
 
         ident = const.tile([P, P], F32, name="ident")
@@ -49,6 +52,7 @@ def tile_cin_pb_v_kernel(tc, h2, x0, W3, b3, pre, grad_out, out_0, out_1):
         x0f = const.tile([P, NT], BF16, name="x0f")
         h2t = const.tile([P, NF * 4], BF16, name="h2t")
         x0t = const.tile([P, NG * 4], BF16, name="x0t")
+        x0s = const.tile([P, NG], F32, name="x0s")
         pre_sb = const.tile([P, 4, NC], F32, name="pre_sb")
         dp_nat = const.tile([P, 4, NC], BF16, name="dp_nat")
         dp_tok = const.tile([P, WIDE], BF16, name="dp_tok", align_bytes=64)
@@ -58,14 +62,16 @@ def tile_cin_pb_v_kernel(tc, h2, x0, W3, b3, pre, grad_out, out_0, out_1):
         dpf_c = const.tile([P, NT], U32, name="dpf_c", align_bytes=64)
         dpf_s = const.tile([P, NT], U8, name="dpf_s", align_bytes=64)
         o0 = const.tile([P, NT], F32, name="o0")
-        acc = []
-        for k in range(8):
-            acc_k = const.tile([P, NF], F32, name="acc%d" % k)
-            acc.append(acc_k)
+        acc = {}
+        for j in range(JS):
+            for s in range(GG):
+                acc_t_ = const.tile([P, NF], F32, name="acc%d_%d" % (j, s))
+                acc[(j, s)] = acc_t_
         w_raw = []
         for i in range(NGRP):
             w_i = const.tile([P, GG, NC], BF16, name="w_raw%d" % i)
             w_raw.append(w_i)
+        accp = ps_ac.tile([P, 512], F32, name="accp")
 
         x0t_v = x0t[:].rearrange("p (g j) -> p g j", j=4)
         h2t_v = h2t[:].rearrange("p (f j) -> p f j", j=4)
@@ -96,6 +102,8 @@ def tile_cin_pb_v_kernel(tc, h2, x0, W3, b3, pre, grad_out, out_0, out_1):
         zs = {}
         zc = {}
         az = {}
+        ots = {}
+        pts = {}
 
         def turn_w(i):
             gw_t = st3.tile([P, WIDE], BF16, name="gw", tag="gw", align_bytes=64)
@@ -108,43 +116,77 @@ def tile_cin_pb_v_kernel(tc, h2, x0, W3, b3, pre, grad_out, out_0, out_1):
             wc[i] = (wc_t, ws_t)
             nc.vector.quantize_mx(out=wc_t[:].bitcast(E4X4), scales=ws_t[:], in_=gw.pop(i)[:])
 
-        def mm_a(i, js):
+        def mm_a(i, j):
             wc_t, ws_t = wc[i]
-            for j in js:
-                az_t = ps_az.tile([P, 512], F32, name="az", tag="az")
-                az[(i, j)] = az_t
-                nc.tensor.matmul_mx(
-                    out=az_t[:],
-                    lhsT=dpf_c[:, P * j : P * (j + 1)].bitcast(E5X4),
-                    lhsT_scale=dpf_s[:, P * j : P * (j + 1)],
-                    rhs=wc_t[:].bitcast(E4X4),
-                    rhs_scale=ws_t[:],
-                    start=True,
-                    stop=True,
-                )
+            az_t = ps_az.tile([P, 512], F32, name="az", tag="az")
+            az[(i, j)] = az_t
+            nc.tensor.matmul_mx(
+                out=az_t[:],
+                lhsT=dpf_c[:, P * j : P * (j + 1)].bitcast(E5X4),
+                lhsT_scale=dpf_s[:, P * j : P * (j + 1)],
+                rhs=wc_t[:].bitcast(E4X4),
+                rhs_scale=ws_t[:],
+                start=True,
+                stop=True,
+            )
 
-        def fold(i, js):
+        def fold(i, j):
+            bank = az.pop((i, j))
             for s in range(GG):
                 g = GG * i + s
-                for j in js:
-                    a_t = acc[4 * (s % 2) + j]
-                    if g < 2:
-                        nc.vector.tensor_scalar(
-                            out=a_t[:],
-                            in0=az[(i, j)][:, P * s : P * (s + 1)],
-                            scalar1=x0t_v[:, g, j : j + 1],
-                            scalar2=None,
-                            op0=MULT,
-                        )
-                    else:
-                        nc.vector.scalar_tensor_tensor(
-                            out=a_t[:],
-                            in0=az[(i, j)][:, P * s : P * (s + 1)],
-                            scalar=x0t_v[:, g, j : j + 1],
-                            in1=a_t[:],
-                            op0=MULT,
-                            op1=ADD,
-                        )
+                if i == 0:
+                    nc.vector.tensor_scalar(
+                        out=acc[(j, s)][:],
+                        in0=bank[:, P * s : P * (s + 1)],
+                        scalar1=x0t_v[:, g, j : j + 1],
+                        scalar2=None,
+                        op0=MULT,
+                    )
+                else:
+                    nc.vector.scalar_tensor_tensor(
+                        out=acc[(j, s)][:],
+                        in0=bank[:, P * s : P * (s + 1)],
+                        scalar=x0t_v[:, g, j : j + 1],
+                        in1=acc[(j, s)][:],
+                        op0=MULT,
+                        op1=ADD,
+                    )
+
+        def scale_s(i):
+            bank = az.pop((i, JS))
+            pt = st2.tile([P, 512], F32, name="pt", tag="pt")
+            pts[i] = pt
+            for s in range(GG):
+                nc.scalar.activation(
+                    out=pt[:, P * s : P * (s + 1)],
+                    in_=bank[:, P * s : P * (s + 1)],
+                    func=COPY,
+                    scale=x0s[:, GG * i + s : GG * i + s + 1],
+                )
+
+        def add_up_s(i):
+            pt = pts.pop(i)
+            for s in range(GG):
+                g = GG * i + s
+                nc.tensor.matmul(
+                    out=accp[:, P * JS : P * (JS + 1)],
+                    lhsT=pt[:, P * s : P * (s + 1)],
+                    rhs=ident[:],
+                    is_transpose=True,
+                    start=(g == 0),
+                    stop=(g == NG - 1),
+                )
+
+        def finish(j):
+            for s in range(GG):
+                nc.tensor.matmul(
+                    out=accp[:, P * j : P * (j + 1)],
+                    lhsT=acc[(j, s)][:],
+                    rhs=ident[:],
+                    is_transpose=True,
+                    start=(s == 0),
+                    stop=(s == GG - 1),
+                )
 
         def make_z_pool(i):
             zs_t = st2.tile([P, WIDE], BF16, name="zs", tag="zs", align_bytes=64)
@@ -171,8 +213,6 @@ def tile_cin_pb_v_kernel(tc, h2, x0, W3, b3, pre, grad_out, out_0, out_1):
             zc[i] = (zc_t, zq_t)
             nc.vector.quantize_mx(out=zc_t[:].bitcast(E4X4), scales=zq_t[:], in_=zs.pop(i)[:])
 
-        ots = {}
-
         def mm_b(i, ss):
             zc_t, zq_t = zc[i]
             if 0 in ss:
@@ -191,19 +231,10 @@ def tile_cin_pb_v_kernel(tc, h2, x0, W3, b3, pre, grad_out, out_0, out_1):
                     stop=True,
                 )
                 nc.scalar.copy(out=ot[:, s, :], in_=bw[:])
-            if GG - 1 in ss:
+                if i == NGRP - 1:
+                    nc.sync.dma_start(out=out1_v[:, GG * i + s, :], in_=ot[:, s, :])
+            if GG - 1 in ss and i < NGRP - 1:
                 nc.sync.dma_start(out=out1_v[:, GG * i : GG * (i + 1), :], in_=ot[:])
-
-        fins = []
-
-        def finish(js):
-            if len(fins) == 0:
-                fin_t = ps_az.tile([P, 512], F32, name="az", tag="az")
-                fins.append(fin_t)
-            for j in js:
-                nc.vector.tensor_tensor(out=acc[j][:], in0=acc[j][:], in1=acc[4 + j][:], op=ADD)
-            for j in js:
-                nc.tensor.transpose(out=fins[0][:, P * j : P * (j + 1)], in_=acc[j][:], identity=ident[:])
 
         make_identity(nc, ident[:])
         nc.vector.memset(gr[:], 0.0)
@@ -223,6 +254,13 @@ def tile_cin_pb_v_kernel(tc, h2, x0, W3, b3, pre, grad_out, out_0, out_1):
         )
         gps = ps_sx.tile([P, 512], F32, name="sx", tag="sx")
         nc.tensor.matmul(out=gps[:], lhsT=spread[:], rhs=gr[:], start=True, stop=True)
+        hx = ps_sx.tile([P, 512], F32, name="sx", tag="sx")
+        h2w = h2f[:].bitcast(F32)
+        x0w = x0f[:].bitcast(F32)
+        for u in range(2):
+            nc.tensor.transpose(out=hx[:, P * u : P * (u + 1)], in_=h2w[:, u:256:2], identity=ident[:])
+        for u in range(2):
+            nc.tensor.transpose(out=hx[:, P * (2 + u) : P * (3 + u)], in_=x0w[:, u:256:2], identity=ident[:])
         for j in range(4):
             nc.vector.scalar_tensor_tensor(
                 out=dp_nat[:, j, :],
@@ -233,19 +271,7 @@ def tile_cin_pb_v_kernel(tc, h2, x0, W3, b3, pre, grad_out, out_0, out_1):
                 op1=MULT,
             )
         turn(dp_nat[:], dp_ftr[:], ps_az, "az")
-        nc.vector.tensor_copy(
-            out=dp_tok[:].rearrange("p (c j) -> p c j", j=4),
-            in_=dp_nat[:].rearrange("p j c -> p c j"),
-        )
-        hx = ps_sx.tile([P, 512], F32, name="sx", tag="sx")
-        h2w = h2f[:].bitcast(F32)
-        x0w = x0f[:].bitcast(F32)
-        for u in range(2):
-            nc.tensor.transpose(out=hx[:, P * u : P * (u + 1)], in_=h2w[:, u:256:2], identity=ident[:])
-        for u in range(2):
-            nc.tensor.transpose(out=hx[:, P * (2 + u) : P * (3 + u)], in_=x0w[:, u:256:2], identity=ident[:])
         turn_w(0)
-        nc.vector.quantize_mx(out=dpf_c[:].bitcast(E5X4), scales=dpf_s[:], in_=dp_ftr[:])
         nc.vector.tensor_copy(
             out=h2t[:].bitcast(F32).rearrange("p (f u) -> p f u", u=2),
             in_=hx[:, 0:256].rearrange("p (u f) -> p f u", u=2),
@@ -254,40 +280,61 @@ def tile_cin_pb_v_kernel(tc, h2, x0, W3, b3, pre, grad_out, out_0, out_1):
             out=x0t[:].bitcast(F32).rearrange("p (g u) -> p g u", u=2),
             in_=hx[:, 256:512].rearrange("p (u f) -> p f u", u=2)[:, 0:NG, :],
         )
+        nc.vector.tensor_copy(out=x0s[:], in_=x0t_v[:, :, JS])
         make_z_pool(0)
         make_z_pool(1)
+        nc.vector.tensor_copy(
+            out=dp_tok[:].rearrange("p (c j) -> p c j", j=4),
+            in_=dp_nat[:].rearrange("p j c -> p c j"),
+        )
+        make_z_vec(0)
+        nc.vector.quantize_mx(out=dpf_c[:].bitcast(E5X4), scales=dpf_s[:], in_=dp_ftr[:])
         nc.vector.quantize_mx(out=dpk_c[:].bitcast(E5X4), scales=dpk_s[:], in_=dp_tok[:])
         turn_w(1)
-        make_z_vec(0)
         quant_w(0)
         quant_z(0)
         make_z_pool(2)
-        mm_a(0, (0, 1))
+        mm_a(0, JS)
+        scale_s(0)
+        mm_a(0, 0)
+        mm_a(0, 1)
 
-        for i in range(NGRP):
+        for i in range(NGRP - 1):
             if i + LOADS_AHEAD < NGRP:
                 load_w(i + LOADS_AHEAD)
-            if i + 1 < NGRP:
-                make_z_vec(i + 1)
-                quant_w(i + 1)
-                quant_z(i + 1)
+            make_z_vec(i + 1)
+            quant_w(i + 1)
+            quant_z(i + 1)
             if i + 3 < NGRP:
                 make_z_pool(i + 3)
             if i + TURNS_AHEAD < NGRP:
                 turn_w(i + TURNS_AHEAD)
+            add_up_s(i)
+            mm_a(i, 2)
             mm_b(i, (0, 1))
-            mm_a(i, (2, 3))
-            mm_b(i, (2, 3))
-            fold(i, (0, 1))
-            if i + 1 < NGRP:
-                mm_a(i + 1, (0, 1))
-            else:
-                finish((0, 1))
-            fold(i, (2, 3))
+            fold(i, 0)
+            mm_a(i + 1, JS)
+            scale_s(i + 1)
+            mm_b(i, (2,))
+            fold(i, 1)
+            mm_a(i + 1, 0)
+            mm_b(i, (3,))
+            fold(i, 2)
+            mm_a(i + 1, 1)
 
-        finish((2, 3))
+        i = NGRP - 1
+        mm_b(i, (0, 1))
+        add_up_s(i)
+        mm_a(i, 2)
+        mm_b(i, (2, 3))
+        fold(i, 0)
+        fold(i, 1)
+        finish(0)
+        finish(1)
+        fold(i, 2)
+        finish(2)
         nc.vector.tensor_copy(
             out=o0[:].rearrange("f (p j) -> f p j", j=4),
-            in_=fins[0][:].rearrange("f (j p) -> f p j", j=4),
+            in_=accp[:].rearrange("f (j p) -> f p j", j=4),
         )
         nc.sync.dma_start(out=out_0.rearrange("b f d -> f b d"), in_=o0[:].rearrange("f (b d) -> f b d", d=ND))

@@ -213,7 +213,7 @@ def tile_cin_pb_v_kernel(tc, h2, x0, W3, b3, pre, grad_out, out_0, out_1):
             zc[i] = (zc_t, zq_t)
             nc.vector.quantize_mx(out=zc_t[:].bitcast(E4X4), scales=zq_t[:], in_=zs.pop(i)[:])
 
-        def mm_b(i, ss):
+        def mm_b(i, ss, on_vector=False):
             zc_t, zq_t = zc[i]
             if 0 in ss:
                 ot_t = st3.tile([P, GG, NC], F32, name="ot", tag="ot")
@@ -230,7 +230,10 @@ def tile_cin_pb_v_kernel(tc, h2, x0, W3, b3, pre, grad_out, out_0, out_1):
                     start=True,
                     stop=True,
                 )
-                nc.scalar.copy(out=ot[:, s, :], in_=bw[:])
+                if on_vector:
+                    nc.vector.tensor_copy(out=ot[:, s, :], in_=bw[:])
+                else:
+                    nc.scalar.copy(out=ot[:, s, :], in_=bw[:])
                 if i == NGRP - 1:
                     nc.sync.dma_start(out=out1_v[:, GG * i + s, :], in_=ot[:, s, :])
             if GG - 1 in ss and i < NGRP - 1:
@@ -261,6 +264,15 @@ def tile_cin_pb_v_kernel(tc, h2, x0, W3, b3, pre, grad_out, out_0, out_1):
             nc.tensor.transpose(out=hx[:, P * u : P * (u + 1)], in_=h2w[:, u:256:2], identity=ident[:])
         for u in range(2):
             nc.tensor.transpose(out=hx[:, P * (2 + u) : P * (3 + u)], in_=x0w[:, u:256:2], identity=ident[:])
+        nc.scalar.copy(
+            out=h2t[:].bitcast(F32).rearrange("p (f u) -> p f u", u=2),
+            in_=hx[:, 0:256].rearrange("p (u f) -> p f u", u=2),
+        )
+        nc.scalar.copy(
+            out=x0t[:].bitcast(F32).rearrange("p (g u) -> p g u", u=2),
+            in_=hx[:, 256:512].rearrange("p (u f) -> p f u", u=2)[:, 0:NG, :],
+        )
+        nc.scalar.copy(out=x0s[:], in_=x0t_v[:, :, JS])
         for j in range(4):
             nc.vector.scalar_tensor_tensor(
                 out=dp_nat[:, j, :],
@@ -272,15 +284,6 @@ def tile_cin_pb_v_kernel(tc, h2, x0, W3, b3, pre, grad_out, out_0, out_1):
             )
         turn(dp_nat[:], dp_ftr[:], ps_az, "az")
         turn_w(0)
-        nc.vector.tensor_copy(
-            out=h2t[:].bitcast(F32).rearrange("p (f u) -> p f u", u=2),
-            in_=hx[:, 0:256].rearrange("p (u f) -> p f u", u=2),
-        )
-        nc.vector.tensor_copy(
-            out=x0t[:].bitcast(F32).rearrange("p (g u) -> p g u", u=2),
-            in_=hx[:, 256:512].rearrange("p (u f) -> p f u", u=2)[:, 0:NG, :],
-        )
-        nc.vector.tensor_copy(out=x0s[:], in_=x0t_v[:, :, JS])
         make_z_pool(0)
         make_z_pool(1)
         nc.vector.tensor_copy(
@@ -299,7 +302,7 @@ def tile_cin_pb_v_kernel(tc, h2, x0, W3, b3, pre, grad_out, out_0, out_1):
         mm_a(0, 0)
         mm_a(0, 1)
 
-        for i in range(NGRP - 1):
+        for i in range(NGRP - 3):
             if i + LOADS_AHEAD < NGRP:
                 load_w(i + LOADS_AHEAD)
             make_z_vec(i + 1)
@@ -307,8 +310,7 @@ def tile_cin_pb_v_kernel(tc, h2, x0, W3, b3, pre, grad_out, out_0, out_1):
             quant_z(i + 1)
             if i + 3 < NGRP:
                 make_z_pool(i + 3)
-            if i + TURNS_AHEAD < NGRP:
-                turn_w(i + TURNS_AHEAD)
+            turn_w(i + TURNS_AHEAD)
             add_up_s(i)
             mm_a(i, 2)
             mm_b(i, (0, 1))
@@ -322,16 +324,52 @@ def tile_cin_pb_v_kernel(tc, h2, x0, W3, b3, pre, grad_out, out_0, out_1):
             fold(i, 2)
             mm_a(i + 1, 1)
 
-        i = NGRP - 1
-        mm_b(i, (0, 1))
+        i = NGRP - 3
+        make_z_vec(i + 1)
+        turn_w(i + 2)
+        fold(i, 0)
+        quant_w(i + 1)
+        fold(i, 1)
         add_up_s(i)
         mm_a(i, 2)
+        mm_b(i, (0,))
+        mm_a(i + 1, 0)
+        mm_b(i, (1,))
+        mm_a(i + 1, JS)
+        scale_s(i + 1)
+        quant_z(i + 1)
+        fold(i, 2)
         mm_b(i, (2, 3))
+        mm_a(i + 1, 1)
+
+        i = NGRP - 2
+        mm_b(i, (0, 1))
+        fold(i, 0)
+        quant_w(i + 1)
+        make_z_vec(i + 1)
+        fold(i, 1)
+        mm_a(i, 2)
+        mm_a(i + 1, 0)
+        mm_b(i, (2, 3))
+        add_up_s(i)
+        quant_z(i + 1)
+        fold(i, 2)
+        mm_a(i + 1, JS)
+        mm_a(i + 1, 1)
+        scale_s(i + 1)
+
+        i = NGRP - 1
         fold(i, 0)
         fold(i, 1)
+        mm_b(i, (0,), on_vector=True)
+        mm_b(i, (1,))
+        mm_a(i, 2)
+        fold(i, 2)
+        mm_b(i, (2,), on_vector=True)
+        mm_b(i, (3,))
+        add_up_s(i)
         finish(0)
         finish(1)
-        fold(i, 2)
         finish(2)
         nc.vector.tensor_copy(
             out=o0[:].rearrange("f (p j) -> f p j", j=4),

from contextlib import ExitStack

import concourse.mybir as mybir
from concourse.masks import make_identity

NB, NF, NG, ND, NC = 16, 128, 64, 32, 512
NT = NB * ND
NK = NF * NG
FLOPS = 2 * 2 * NT * NC * NK
BYTES = 2 * (NB * NF * ND + NB * NG * ND + NK * NC + NB * NC) + 4 * (NT * NC + NB * NF * ND + NK * NC)

F32 = mybir.dt.float32
BF16 = mybir.dt.bfloat16
U32 = mybir.dt.uint32
U8 = mybir.dt.uint8
E4X4 = mybir.dt.float8_e4m3fn_x4
E5X4 = mybir.dt.float8_e5m2_x4
MULT = mybir.AluOpType.mult
ADD = mybir.AluOpType.add
IS_GT = mybir.AluOpType.is_gt
COPY = mybir.ActivationFunctionType.Copy

P = 128
GG = 4
NGRP = NG // GG
WIDE = GG * P * 4
LOADS_AHEAD = 8
TURNS_AHEAD = 2
GV = 3
JS = 3


def tile_cin_pb_v_kernel(tc, h2, x0, W3, b3, pre, grad_out, out_0, out_1):
    nc = tc.nc
    w3_v = W3.rearrange("(f g) c -> f g c", g=NG)
    out1_v = out_1.rearrange("(f g) c -> f g c", g=NG)
    pre_v = pre.rearrange("b (q j) c -> (b q) j c", j=4)

    with ExitStack() as ctx:
        const = ctx.enter_context(tc.tile_pool(name="const", bufs=1))
        st3 = ctx.enter_context(tc.tile_pool(name="st3", bufs=3))
        st2 = ctx.enter_context(tc.tile_pool(name="st2", bufs=2))
        ps_sx = ctx.enter_context(tc.psum_pool(name="ps_sx", bufs=4))
        ps_az = ctx.enter_context(tc.psum_pool(name="ps_az", bufs=3))
        ps_ac = ctx.enter_context(tc.psum_pool(name="ps_ac", bufs=1))
        ctx.enter_context(tc.manual_schedule())

        ident = const.tile([P, P], F32, name="ident")
        spread = const.tile([P, P], BF16, name="spread")
        gr = const.tile([P, NC], BF16, name="gr")
        h2f = const.tile([P, NT], BF16, name="h2f")
        x0f = const.tile([P, NT], BF16, name="x0f")
        h2t = const.tile([P, NF * 4], BF16, name="h2t")
        x0t = const.tile([P, NG * 4], BF16, name="x0t")
        x0s = const.tile([P, NG], F32, name="x0s")
        pre_sb = const.tile([P, 4, NC], F32, name="pre_sb")
        dp_nat = const.tile([P, 4, NC], BF16, name="dp_nat")
        dp_tok = const.tile([P, WIDE], BF16, name="dp_tok", align_bytes=64)
        dp_ftr = const.tile([P, WIDE], BF16, name="dp_ftr", align_bytes=64)
        dpk_c = const.tile([P, NC], U32, name="dpk_c", align_bytes=64)
        dpk_s = const.tile([P, NC], U8, name="dpk_s", align_bytes=64)
        dpf_c = const.tile([P, NT], U32, name="dpf_c", align_bytes=64)
        dpf_s = const.tile([P, NT], U8, name="dpf_s", align_bytes=64)
        o0 = const.tile([P, NT], F32, name="o0")
        acc = {}
        for j in range(JS):
            for s in range(GG):
                acc_t_ = const.tile([P, NF], F32, name="acc%d_%d" % (j, s))
                acc[(j, s)] = acc_t_
        w_raw = []
        for i in range(NGRP):
            w_i = const.tile([P, GG, NC], BF16, name="w_raw%d" % i)
            w_raw.append(w_i)
        accp = ps_ac.tile([P, 512], F32, name="accp")

        x0t_v = x0t[:].rearrange("p (g j) -> p g j", j=4)
        h2t_v = h2t[:].rearrange("p (f j) -> p f j", j=4)

        def load_w(i):
            nc.sync.dma_start(out=w_raw[i][:], in_=w3_v[:, GG * i : GG * (i + 1), :])

        def turn(src, dst, pool, tag):
            words = src.rearrange("p g c -> p (g c)").bitcast(F32)
            dwords = dst.bitcast(F32)
            for h in range(2):
                bank = pool.tile([P, 512], F32, name=tag, tag=tag)
                for k in range(4):
                    g = 2 * h + k // 2
                    u = k % 2
                    nc.tensor.transpose(
                        out=bank[:, P * k : P * (k + 1)],
                        in_=words[:, 256 * g + u : 256 * (g + 1) : 2],
                        identity=ident[:],
                    )
                nc.scalar.copy(
                    out=dwords[:, 512 * h : 512 * (h + 1)].rearrange("q (g f u) -> q g f u", g=2, u=2),
                    in_=bank[:].rearrange("q (g u f) -> q g f u", g=2, u=2),
                )

        gw = {}
        wc = {}
        zs = {}
        zc = {}
        az = {}
        ots = {}
        pts = {}

        def turn_w(i):
            gw_t = st3.tile([P, WIDE], BF16, name="gw", tag="gw", align_bytes=64)
            gw[i] = gw_t
            turn(w_raw[i][:], gw_t[:], ps_sx, "sx")

        def quant_w(i):
            wc_t = st2.tile([P, 512], U32, name="wc", tag="wc", align_bytes=64)
            ws_t = st2.tile([P, 512], U8, name="ws", tag="ws", align_bytes=64)
            wc[i] = (wc_t, ws_t)
            nc.vector.quantize_mx(out=wc_t[:].bitcast(E4X4), scales=ws_t[:], in_=gw.pop(i)[:])

        def mm_a(i, j):
            wc_t, ws_t = wc[i]
            az_t = ps_az.tile([P, 512], F32, name="az", tag="az")
            az[(i, j)] = az_t
            nc.tensor.matmul_mx(
                out=az_t[:],
                lhsT=dpf_c[:, P * j : P * (j + 1)].bitcast(E5X4),
                lhsT_scale=dpf_s[:, P * j : P * (j + 1)],
                rhs=wc_t[:].bitcast(E4X4),
                rhs_scale=ws_t[:],
                start=True,
                stop=True,
            )

        def fold(i, j):
            bank = az.pop((i, j))
            for s in range(GG):
                g = GG * i + s
                if i == 0:
                    nc.vector.tensor_scalar(
                        out=acc[(j, s)][:],
                        in0=bank[:, P * s : P * (s + 1)],
                        scalar1=x0t_v[:, g, j : j + 1],
                        scalar2=None,
                        op0=MULT,
                    )
                else:
                    nc.vector.scalar_tensor_tensor(
                        out=acc[(j, s)][:],
                        in0=bank[:, P * s : P * (s + 1)],
                        scalar=x0t_v[:, g, j : j + 1],
                        in1=acc[(j, s)][:],
                        op0=MULT,
                        op1=ADD,
                    )

        def scale_s(i):
            bank = az.pop((i, JS))
            pt = st2.tile([P, 512], F32, name="pt", tag="pt")
            pts[i] = pt
            for s in range(GG):
                nc.scalar.activation(
                    out=pt[:, P * s : P * (s + 1)],
                    in_=bank[:, P * s : P * (s + 1)],
                    func=COPY,
                    scale=x0s[:, GG * i + s : GG * i + s + 1],
                )

        def add_up_s(i):
            pt = pts.pop(i)
            for s in range(GG):
                g = GG * i + s
                nc.tensor.matmul(
                    out=accp[:, P * JS : P * (JS + 1)],
                    lhsT=pt[:, P * s : P * (s + 1)],
                    rhs=ident[:],
                    is_transpose=True,
                    start=(g == 0),
                    stop=(g == NG - 1),
                )

        def finish(j):
            for s in range(GG):
                nc.tensor.matmul(
                    out=accp[:, P * j : P * (j + 1)],
                    lhsT=acc[(j, s)][:],
                    rhs=ident[:],
                    is_transpose=True,
                    start=(s == 0),
                    stop=(s == GG - 1),
                )

        def make_z_pool(i):
            zs_t = st2.tile([P, WIDE], BF16, name="zs", tag="zs", align_bytes=64)
            zs[i] = zs_t
            for s in range(GV, GG):
                nc.gpsimd.tensor_tensor(
                    out=zs_t[:, 4 * P * s : 4 * P * (s + 1)].rearrange("p (f j) -> p f j", j=4),
                    in0=x0t_v[:, GG * i + s, :].unsqueeze(1).to_broadcast([P, NF, 4]),
                    in1=h2t_v,
                    op=MULT,
                )

        def make_z_vec(i):
            nc.vector.tensor_tensor(
                out=zs[i][:, 0 : 4 * P * GV].rearrange("p (g f j) -> p g f j", g=GV, j=4),
                in0=x0t_v[:, GG * i : GG * i + GV, :].unsqueeze(2).to_broadcast([P, GV, NF, 4]),
                in1=h2t_v.unsqueeze(1).to_broadcast([P, GV, NF, 4]),
                op=MULT,
            )

        def quant_z(i):
            zc_t = st3.tile([P, 512], U32, name="zc", tag="zc", align_bytes=64)
            zq_t = st3.tile([P, 512], U8, name="zq", tag="zq", align_bytes=64)
            zc[i] = (zc_t, zq_t)
            nc.vector.quantize_mx(out=zc_t[:].bitcast(E4X4), scales=zq_t[:], in_=zs.pop(i)[:])

        def mm_b(i, ss, on_vector=False):
            zc_t, zq_t = zc[i]
            if 0 in ss:
                ot_t = st3.tile([P, GG, NC], F32, name="ot", tag="ot")
                ots[i] = ot_t
            ot = ots[i]
            for s in ss:
                bw = ps_sx.tile([P, 512], F32, name="sx", tag="sx")
                nc.tensor.matmul_mx(
                    out=bw[:],
                    lhsT=zc_t[:, P * s : P * (s + 1)].bitcast(E4X4),
                    lhsT_scale=zq_t[:, P * s : P * (s + 1)],
                    rhs=dpk_c[:].bitcast(E5X4),
                    rhs_scale=dpk_s[:],
                    start=True,
                    stop=True,
                )
                if on_vector:
                    nc.vector.tensor_copy(out=ot[:, s, :], in_=bw[:])
                else:
                    nc.scalar.copy(out=ot[:, s, :], in_=bw[:])
                if i == NGRP - 1:
                    nc.sync.dma_start(out=out1_v[:, GG * i + s, :], in_=ot[:, s, :])
            if GG - 1 in ss and i < NGRP - 1:
                nc.sync.dma_start(out=out1_v[:, GG * i : GG * (i + 1), :], in_=ot[:])

        make_identity(nc, ident[:])
        nc.vector.memset(gr[:], 0.0)
        x0_v = x0.rearrange("b g d -> g b d")
        nc.scalar.dma_start(out=x0f[0:NG, :].rearrange("g (b d) -> g b d", d=ND), in_=x0_v)
        nc.scalar.dma_start(out=x0f[NG:P, :].rearrange("g (b d) -> g b d", d=ND), in_=x0_v)
        nc.scalar.dma_start(out=h2f[:].rearrange("f (b d) -> f b d", d=ND), in_=h2.rearrange("b f d -> f b d"))
        nc.sync.dma_start(out=gr[0:NB, :], in_=grad_out)
        for j in range(4):
            nc.sync.dma_start(out=pre_sb[:, j, :], in_=pre_v[:, j, :])
        for i in range(LOADS_AHEAD):
            load_w(i)

        nc.vector.tensor_copy(
            out=spread[:].rearrange("k (b r) -> k b r", r=8),
            in_=ident[:, 0:NB].unsqueeze(2).to_broadcast([P, NB, 8]),
        )
        gps = ps_sx.tile([P, 512], F32, name="sx", tag="sx")
        nc.tensor.matmul(out=gps[:], lhsT=spread[:], rhs=gr[:], start=True, stop=True)
        hx = ps_sx.tile([P, 512], F32, name="sx", tag="sx")
        h2w = h2f[:].bitcast(F32)
        x0w = x0f[:].bitcast(F32)
        for u in range(2):
            nc.tensor.transpose(out=hx[:, P * u : P * (u + 1)], in_=h2w[:, u:256:2], identity=ident[:])
        for u in range(2):
            nc.tensor.transpose(out=hx[:, P * (2 + u) : P * (3 + u)], in_=x0w[:, u:256:2], identity=ident[:])
        nc.scalar.copy(
            out=h2t[:].bitcast(F32).rearrange("p (f u) -> p f u", u=2),
            in_=hx[:, 0:256].rearrange("p (u f) -> p f u", u=2),
        )
        nc.scalar.copy(
            out=x0t[:].bitcast(F32).rearrange("p (g u) -> p g u", u=2),
            in_=hx[:, 256:512].rearrange("p (u f) -> p f u", u=2)[:, 0:NG, :],
        )
        nc.scalar.copy(out=x0s[:], in_=x0t_v[:, :, JS])
        for j in range(4):
            nc.vector.scalar_tensor_tensor(
                out=dp_nat[:, j, :],
                in0=pre_sb[:, j, :],
                scalar=0.0,
                in1=gps[:],
                op0=IS_GT,
                op1=MULT,
            )
        turn(dp_nat[:], dp_ftr[:], ps_az, "az")
        turn_w(0)
        make_z_pool(0)
        make_z_pool(1)
        nc.vector.tensor_copy(
            out=dp_tok[:].rearrange("p (c j) -> p c j", j=4),
            in_=dp_nat[:].rearrange("p j c -> p c j"),
        )
        make_z_vec(0)
        nc.vector.quantize_mx(out=dpf_c[:].bitcast(E5X4), scales=dpf_s[:], in_=dp_ftr[:])
        nc.vector.quantize_mx(out=dpk_c[:].bitcast(E5X4), scales=dpk_s[:], in_=dp_tok[:])
        turn_w(1)
        quant_w(0)
        quant_z(0)
        make_z_pool(2)
        mm_a(0, JS)
        scale_s(0)
        mm_a(0, 0)
        mm_a(0, 1)

        for i in range(NGRP - 3):
            if i + LOADS_AHEAD < NGRP:
                load_w(i + LOADS_AHEAD)
            make_z_vec(i + 1)
            quant_w(i + 1)
            quant_z(i + 1)
            if i + 3 < NGRP:
                make_z_pool(i + 3)
            turn_w(i + TURNS_AHEAD)
            add_up_s(i)
            mm_a(i, 2)
            mm_b(i, (0, 1))
            fold(i, 0)
            mm_a(i + 1, JS)
            scale_s(i + 1)
            mm_b(i, (2,))
            fold(i, 1)
            mm_a(i + 1, 0)
            mm_b(i, (3,))
            fold(i, 2)
            mm_a(i + 1, 1)

        i = NGRP - 3
        make_z_vec(i + 1)
        turn_w(i + 2)
        fold(i, 0)
        quant_w(i + 1)
        fold(i, 1)
        add_up_s(i)
        mm_a(i, 2)
        mm_b(i, (0,))
        mm_a(i + 1, 0)
        mm_b(i, (1,))
        mm_a(i + 1, JS)
        scale_s(i + 1)
        quant_z(i + 1)
        fold(i, 2)
        mm_b(i, (2, 3))
        mm_a(i + 1, 1)

        i = NGRP - 2
        mm_b(i, (0, 1))
        fold(i, 0)
        quant_w(i + 1)
        make_z_vec(i + 1)
        fold(i, 1)
        mm_a(i, 2)
        mm_a(i + 1, 0)
        mm_b(i, (2, 3))
        add_up_s(i)
        quant_z(i + 1)
        fold(i, 2)
        mm_a(i + 1, JS)
        mm_a(i + 1, 1)
        scale_s(i + 1)

        i = NGRP - 1
        fold(i, 0)
        fold(i, 1)
        mm_b(i, (0,), on_vector=True)
        mm_b(i, (1,))
        mm_a(i, 2)
        fold(i, 2)
        mm_b(i, (2,), on_vector=True)
        mm_b(i, (3,))
        add_up_s(i)
        finish(0)
        finish(1)
        finish(2)
        nc.vector.tensor_copy(
            out=o0[:].rearrange("f (p j) -> f p j", j=4),
            in_=accp[:].rearrange("f (j p) -> f p j", j=4),
        )
        nc.sync.dma_start(out=out_0.rearrange("b f d -> f b d"), in_=o0[:].rearrange("f (b d) -> f b d", d=ND))
